import numpy as np
import ml_dtypes

BF16 = ml_dtypes.bfloat16


def bf(x):
    return np.asarray(x, np.float32).astype(BF16)


def f32(x):
    return np.asarray(x, np.float32)


def f64(x):
    return np.asarray(x).astype(np.float64)


def striped(idx):
    return np.tile(idx.reshape(-1, 16).T, (8, 1))


C, S, N = 128, 2048, 1024
ALPHA = 0.8


def sigmoid(v):
    return 1.0 / (1.0 + np.exp(-v))


def setup_inputs():
    return {"pe": f32(bf(np.random.standard_normal((C, S)))), "w": bf(np.random.standard_normal((C, C)) / np.sqrt(C)), "b": f32(0.5 * np.random.standard_normal((C, 1))), "adj": bf(2.0 * np.random.standard_normal((S, N)) / np.sqrt(S)), "offs": striped(np.random.permutation(S)[:N])}


def reference(pe, w, b, adj, offs):
    idx = offs[:16].T.reshape(-1)
    p = f64(pe)
    h = p * sigmoid(f64(w).T @ p + f64(b))
    return h[:, idx] + (ALPHA / 2.0) * (h @ f64(adj))

@@ -1,0 +1,85 @@
+import concourse.mybir as mybir
+from concourse.masks import make_identity
+
+F32 = mybir.dt.float32
+BF16 = mybir.dt.bfloat16
+U16 = mybir.dt.uint16
+ADD = mybir.AluOpType.add
+MULT = mybir.AluOpType.mult
+SIGMOID = mybir.ActivationFunctionType.Sigmoid
+COPY = mybir.ActivationFunctionType.Copy
+
+P = 128
+S = 2048
+N = 1024
+STEP = 0.4
+BANK = 512
+CHUNKS = S // BANK
+BLOCKS = BANK // P
+HALVES = N // BANK
+
+FLOPS = 2 * P * P * S + 2 * P * S * N
+
+
+def tile_hode_mdp_kernel(tc, pe, w, b, adj, offs, out):
+    nc = tc.nc
+    with (
+        tc.tile_pool(name="held", bufs=1) as held,
+        tc.tile_pool(name="work", bufs=2) as work,
+        tc.psum_pool(name="gate_banks", bufs=2) as gate_banks,
+        tc.psum_pool(name="flip_banks", bufs=2) as flip_banks,
+        tc.psum_pool(name="sum_banks", bufs=1) as sum_banks,
+    ):
+        offsets = held.tile([P, N // 16], U16, name="offsets")
+        nc.sync.dma_start(offsets[:], offs)
+        w_sb = held.tile([P, P], BF16, name="w_sb")
+        nc.scalar.dma_start(w_sb[:], w)
+        b_sb = held.tile([P, 1], F32, name="b_sb")
+        nc.scalar.dma_start(b_sb[:], b)
+        pe_sb = [held.tile([P, BANK], F32, name=f"pe{c}") for c in range(CHUNKS)]
+        for c in range(CHUNKS):
+            nc.sync.dma_start(pe_sb[c][:], pe[:, c * BANK : (c + 1) * BANK])
+        adj_sb = [held.tile([P, N], BF16, name=f"adj{k}") for k in range(S // P)]
+        for k in range(S // P):
+            nc.sync.dma_start(adj_sb[k][:], adj[k * P : (k + 1) * P, :])
+
+        identity = held.tile([P, P], F32, name="identity")
+        make_identity(nc, identity[:])
+
+        h = held.tile([P, S], F32, name="h")
+        sums = [sum_banks.tile([P, BANK], F32, name=f"sum{half}") for half in range(HALVES)]
+
+        for c in range(CHUNKS):
+            pe_bf = work.tile([P, BANK], BF16, name="pe_bf")
+            nc.vector.tensor_copy(pe_bf[:], pe_sb[c][:])
+            gate = gate_banks.tile([P, BANK], F32, name="gate")
+            nc.tensor.matmul(gate[:], w_sb[:], pe_bf[:], start=True, stop=True)
+            sig = work.tile([P, BANK], F32, name="sig")
+            nc.scalar.activation(sig[:], gate[:], SIGMOID, bias=b_sb[:], scale=1.0)
+            nc.vector.tensor_tensor(h[:, c * BANK : (c + 1) * BANK], pe_sb[c][:], sig[:], MULT)
+
+            flipped = flip_banks.tile([P, BANK], F32, name="flipped")
+            for r in range(BLOCKS):
+                q0 = c * BANK + r * P
+                nc.tensor.transpose(flipped[:, r * P : (r + 1) * P], h[:, q0 : q0 + P], identity[:])
+            h_t = work.tile([P, BANK], BF16, name="h_t")
+            nc.scalar.copy(h_t[:], flipped[:])
+
+            for half in range(HALVES):
+                for r in range(BLOCKS):
+                    k = c * BLOCKS + r
+                    nc.tensor.matmul(
+                        sums[half][:],
+                        h_t[:, r * P : (r + 1) * P],
+                        adj_sb[k][:, half * BANK : (half + 1) * BANK],
+                        start=(k == 0),
+                        stop=(k == S // P - 1),
+                    )
+
+        for half in range(HALVES):
+            term = work.tile([P, BANK], F32, name="term")
+            nc.scalar.activation(term[:], sums[half][:], COPY, scale=STEP)
+            result = work.tile([P, BANK], F32, name="result")
+            piece = offsets[:, half * (BANK // 16) : (half + 1) * (BANK // 16)]
+            nc.vector.tensor_tensor(result[:], h[:].indirect(piece), term[:], ADD)
+            nc.sync.dma_start(out[:, half * BANK : (half + 1) * BANK], result[:])

@@ -17,6 +17,7 @@ BANK = 512
 CHUNKS = S // BANK
 BLOCKS = BANK // P
 HALVES = N // BANK
+WARM_UPS = 5
 
 FLOPS = 2 * P * P * S + 2 * P * S * N
 
@@ -30,6 +31,12 @@ def tile_hode_mdp_kernel(tc, pe, w, b, adj, offs, out):
         tc.psum_pool(name="flip_banks", bufs=2) as flip_banks,
         tc.psum_pool(name="sum_banks", bufs=1) as sum_banks,
     ):
+        zeros = held.tile([P, BANK], BF16, name="zeros")
+        nc.vector.memset(zeros[:], 0.0)
+        unused = sum_banks.tile([P, BANK], F32, name="unused")
+        for warm_up in range(WARM_UPS):
+            nc.tensor.matmul(unused[:], zeros[:, 0:P], zeros[:], start=True, stop=True)
+
         offsets = held.tile([P, N // 16], U16, name="offsets")
         nc.sync.dma_start(offsets[:], offs)
         w_sb = held.tile([P, P], BF16, name="w_sb")

@@ -13,11 +13,14 @@ P = 128
 S = 2048
 N = 1024
 STEP = 0.4
-BANK = 512
-CHUNKS = S // BANK
-BLOCKS = BANK // P
-HALVES = N // BANK
-WARM_UPS = 5
+CHUNK = 256
+CHUNKS = S // CHUNK
+BLOCKS = CHUNK // P
+PIECE = 256
+PIECES = N // PIECE
+K_BLOCKS = S // P
+LATE_BLOCKS = 6
+EARLY_BLOCKS = K_BLOCKS - LATE_BLOCKS
 
 FLOPS = 2 * P * P * S + 2 * P * S * N
 
@@ -26,67 +29,88 @@ def tile_hode_mdp_kernel(tc, pe, w, b, adj, offs, out):
     nc = tc.nc
     with (
         tc.tile_pool(name="held", bufs=1) as held,
-        tc.tile_pool(name="work", bufs=2) as work,
         tc.psum_pool(name="gate_banks", bufs=2) as gate_banks,
         tc.psum_pool(name="flip_banks", bufs=2) as flip_banks,
         tc.psum_pool(name="sum_banks", bufs=1) as sum_banks,
     ):
-        zeros = held.tile([P, BANK], BF16, name="zeros")
-        nc.vector.memset(zeros[:], 0.0)
-        unused = sum_banks.tile([P, BANK], F32, name="unused")
-        for warm_up in range(WARM_UPS):
-            nc.tensor.matmul(unused[:], zeros[:, 0:P], zeros[:], start=True, stop=True)
-
         offsets = held.tile([P, N // 16], U16, name="offsets")
         nc.sync.dma_start(offsets[:], offs)
         w_sb = held.tile([P, P], BF16, name="w_sb")
         nc.scalar.dma_start(w_sb[:], w)
         b_sb = held.tile([P, 1], F32, name="b_sb")
         nc.scalar.dma_start(b_sb[:], b)
-        pe_sb = [held.tile([P, BANK], F32, name=f"pe{c}") for c in range(CHUNKS)]
+        pe_sb = [held.tile([P, CHUNK], F32, name=f"pe{c}") for c in range(CHUNKS)]
         for c in range(CHUNKS):
-            nc.sync.dma_start(pe_sb[c][:], pe[:, c * BANK : (c + 1) * BANK])
-        adj_sb = [held.tile([P, N], BF16, name=f"adj{k}") for k in range(S // P)]
-        for k in range(S // P):
+            nc.sync.dma_start(pe_sb[c][:], pe[:, c * CHUNK : (c + 1) * CHUNK])
+        adj_sb = [held.tile([P, N], BF16, name=f"adj{k}") for k in range(K_BLOCKS)]
+        for k in range(K_BLOCKS):
             nc.sync.dma_start(adj_sb[k][:], adj[k * P : (k + 1) * P, :])
 
-        identity = held.tile([P, P], F32, name="identity")
+        identity = held.tile([P, P], BF16, name="identity")
         make_identity(nc, identity[:])
 
         h = held.tile([P, S], F32, name="h")
-        sums = [sum_banks.tile([P, BANK], F32, name=f"sum{half}") for half in range(HALVES)]
+        sig = [held.tile([P, CHUNK], F32, name=f"sig{c}") for c in range(CHUNKS)]
+        h_bf = [held.tile([P, CHUNK], BF16, name=f"h_bf{c}") for c in range(CHUNKS)]
+        h_t = [held.tile([P, CHUNK], BF16, name=f"h_t{c}") for c in range(CHUNKS)]
+        sums = [sum_banks.tile([P, PIECE], F32, name=f"sum{piece}") for piece in range(PIECES)]
 
-        for c in range(CHUNKS):
-            pe_bf = work.tile([P, BANK], BF16, name="pe_bf")
-            nc.vector.tensor_copy(pe_bf[:], pe_sb[c][:])
-            gate = gate_banks.tile([P, BANK], F32, name="gate")
-            nc.tensor.matmul(gate[:], w_sb[:], pe_bf[:], start=True, stop=True)
-            sig = work.tile([P, BANK], F32, name="sig")
-            nc.scalar.activation(sig[:], gate[:], SIGMOID, bias=b_sb[:], scale=1.0)
-            nc.vector.tensor_tensor(h[:, c * BANK : (c + 1) * BANK], pe_sb[c][:], sig[:], MULT)
+        def gate(c):
+            halves = pe_sb[c][:].bitcast(BF16).rearrange("p (s two) -> p s two", two=2)
+            gate_ps = gate_banks.tile([P, CHUNK], F32, name="gate_ps")
+            nc.tensor.matmul(gate_ps[:], w_sb[:], halves[:, :, 1], start=True, stop=True)
+            nc.scalar.activation(sig[c][:], gate_ps[:], SIGMOID, bias=b_sb[:], scale=1.0)
 
-            flipped = flip_banks.tile([P, BANK], F32, name="flipped")
+        def multiply(c):
+            nc.vector.tensor_tensor(h_bf[c][:], pe_sb[c][:], sig[c][:], MULT)
+
+        def fill_window(c):
+            nc.vector.tensor_tensor(h[:, c * CHUNK : (c + 1) * CHUNK], pe_sb[c][:], sig[c][:], MULT)
+
+        def flip(c):
+            flipped = flip_banks.tile([P, CHUNK], BF16, name="flipped")
             for r in range(BLOCKS):
-                q0 = c * BANK + r * P
-                nc.tensor.transpose(flipped[:, r * P : (r + 1) * P], h[:, q0 : q0 + P], identity[:])
-            h_t = work.tile([P, BANK], BF16, name="h_t")
-            nc.scalar.copy(h_t[:], flipped[:])
+                nc.tensor.transpose(flipped[:, r * P : (r + 1) * P], h_bf[c][:, r * P : (r + 1) * P], identity[:])
+            nc.scalar.copy(h_t[c][:], flipped[:])
 
-            for half in range(HALVES):
-                for r in range(BLOCKS):
-                    k = c * BLOCKS + r
-                    nc.tensor.matmul(
-                        sums[half][:],
-                        h_t[:, r * P : (r + 1) * P],
-                        adj_sb[k][:, half * BANK : (half + 1) * BANK],
-                        start=(k == 0),
-                        stop=(k == S // P - 1),
-                    )
+        zeros = held.tile([P, PIECE], BF16, name="zeros")
+        nc.vector.memset(zeros[:], 0.0)
 
-        for half in range(HALVES):
-            term = work.tile([P, BANK], F32, name="term")
-            nc.scalar.activation(term[:], sums[half][:], COPY, scale=STEP)
-            result = work.tile([P, BANK], F32, name="result")
-            piece = offsets[:, half * (BANK // 16) : (half + 1) * (BANK // 16)]
-            nc.vector.tensor_tensor(result[:], h[:].indirect(piece), term[:], ADD)
-            nc.sync.dma_start(out[:, half * BANK : (half + 1) * BANK], result[:])
+        def warm_up():
+            for piece in range(PIECES):
+                nc.tensor.matmul(sums[piece][:], zeros[:, 0:P], zeros[:], start=True, stop=True)
+
+        def add_to_sum(k, piece):
+            c, r = divmod(k, BLOCKS)
+            nc.tensor.matmul(
+                sums[piece][:],
+                h_t[c][:, r * P : (r + 1) * P],
+                adj_sb[k][:, piece * PIECE : (piece + 1) * PIECE],
+                start=(k == 0),
+                stop=(k == K_BLOCKS - 1),
+            )
+
+        for t in range(max(CHUNKS + 5, EARLY_BLOCKS + 4)):
+            if 0 <= t - 3 < CHUNKS:
+                flip(t - 3)
+            if 0 <= t - 1 < CHUNKS:
+                gate(t - 1)
+            if 0 <= t - 2 < CHUNKS:
+                multiply(t - 2)
+            if t < 3:
+                warm_up()
+            if 0 <= t - 4 < EARLY_BLOCKS:
+                for piece in range(PIECES):
+                    add_to_sum(t - 4, piece)
+            if 0 <= t - 5 < CHUNKS:
+                fill_window(t - 5)
+
+        for piece in range(PIECES):
+            for k in range(EARLY_BLOCKS, K_BLOCKS):
+                add_to_sum(k, piece)
+            term = held.tile([P, PIECE], F32, name=f"term{piece}")
+            nc.scalar.activation(term[:], sums[piece][:], COPY, scale=STEP)
+            result = held.tile([P, PIECE], F32, name=f"result{piece}")
+            listed = offsets[:, piece * (PIECE // 16) : (piece + 1) * (PIECE // 16)]
+            nc.vector.tensor_tensor(result[:], h[:].indirect(listed), term[:], ADD)
+            nc.sync.dma_start(out[:, piece * PIECE : (piece + 1) * PIECE], result[:])

@@ -21,6 +21,8 @@ PIECES = N // PIECE
 K_BLOCKS = S // P
 LATE_BLOCKS = 6
 EARLY_BLOCKS = K_BLOCKS - LATE_BLOCKS
+CUT_BLOCKS = 3
+WHOLE_BLOCKS = K_BLOCKS - CUT_BLOCKS
 
 FLOPS = 2 * P * P * S + 2 * P * S * N
 
@@ -42,9 +44,13 @@ def tile_hode_mdp_kernel(tc, pe, w, b, adj, offs, out):
         pe_sb = [held.tile([P, CHUNK], F32, name=f"pe{c}") for c in range(CHUNKS)]
         for c in range(CHUNKS):
             nc.sync.dma_start(pe_sb[c][:], pe[:, c * CHUNK : (c + 1) * CHUNK])
-        adj_sb = [held.tile([P, N], BF16, name=f"adj{k}") for k in range(K_BLOCKS)]
-        for k in range(K_BLOCKS):
+        adj_sb = [held.tile([P, N], BF16, name=f"adj{k}") for k in range(WHOLE_BLOCKS)]
+        for k in range(WHOLE_BLOCKS):
             nc.sync.dma_start(adj_sb[k][:], adj[k * P : (k + 1) * P, :])
+        cut_rows = adj[WHOLE_BLOCKS * P :, :].rearrange("(l p) j -> p l j", p=P)
+        adj_cut = [held.tile([P, CUT_BLOCKS, PIECE], BF16, name=f"adj_cut{piece}") for piece in range(PIECES)]
+        for piece in range(PIECES):
+            nc.sync.dma_start(adj_cut[piece][:], cut_rows[:, :, piece * PIECE : (piece + 1) * PIECE])
 
         identity = held.tile([P, P], BF16, name="identity")
         make_identity(nc, identity[:])
@@ -82,10 +88,14 @@ def tile_hode_mdp_kernel(tc, pe, w, b, adj, offs, out):
 
         def add_to_sum(k, piece):
             c, r = divmod(k, BLOCKS)
+            if k < WHOLE_BLOCKS:
+                adj_part = adj_sb[k][:, piece * PIECE : (piece + 1) * PIECE]
+            else:
+                adj_part = adj_cut[piece][:, k - WHOLE_BLOCKS, :]
             nc.tensor.matmul(
                 sums[piece][:],
                 h_t[c][:, r * P : (r + 1) * P],
-                adj_sb[k][:, piece * PIECE : (piece + 1) * PIECE],
+                adj_part,
                 start=(k == 0),
                 stop=(k == K_BLOCKS - 1),
             )

@@ -19,10 +19,9 @@ BLOCKS = CHUNK // P
 PIECE = 256
 PIECES = N // PIECE
 K_BLOCKS = S // P
-LATE_BLOCKS = 6
-EARLY_BLOCKS = K_BLOCKS - LATE_BLOCKS
-CUT_BLOCKS = 3
-WHOLE_BLOCKS = K_BLOCKS - CUT_BLOCKS
+LATE_CHUNKS = 2
+WHOLE_CHUNKS = CHUNKS - LATE_CHUNKS
+EARLY_BLOCKS = WHOLE_CHUNKS * BLOCKS
 
 FLOPS = 2 * P * P * S + 2 * P * S * N
 
@@ -44,13 +43,14 @@ def tile_hode_mdp_kernel(tc, pe, w, b, adj, offs, out):
         pe_sb = [held.tile([P, CHUNK], F32, name=f"pe{c}") for c in range(CHUNKS)]
         for c in range(CHUNKS):
             nc.sync.dma_start(pe_sb[c][:], pe[:, c * CHUNK : (c + 1) * CHUNK])
-        adj_sb = [held.tile([P, N], BF16, name=f"adj{k}") for k in range(WHOLE_BLOCKS)]
-        for k in range(WHOLE_BLOCKS):
-            nc.sync.dma_start(adj_sb[k][:], adj[k * P : (k + 1) * P, :])
-        cut_rows = adj[WHOLE_BLOCKS * P :, :].rearrange("(l p) j -> p l j", p=P)
-        adj_cut = [held.tile([P, CUT_BLOCKS, PIECE], BF16, name=f"adj_cut{piece}") for piece in range(PIECES)]
+        adj_sb = [held.tile([P, BLOCKS, N], BF16, name=f"adj{c}") for c in range(WHOLE_CHUNKS)]
+        for c in range(WHOLE_CHUNKS):
+            rows = adj[c * CHUNK : (c + 1) * CHUNK, :]
+            nc.sync.dma_start(adj_sb[c][:], rows.rearrange("(p r) j -> p r j", r=BLOCKS))
+        late_rows = adj[WHOLE_CHUNKS * CHUNK :, :].rearrange("(k p) j -> p k j", p=P)
+        adj_cut = [held.tile([P, LATE_CHUNKS * BLOCKS, PIECE], BF16, name=f"adj_cut{piece}") for piece in range(PIECES)]
         for piece in range(PIECES):
-            nc.sync.dma_start(adj_cut[piece][:], cut_rows[:, :, piece * PIECE : (piece + 1) * PIECE])
+            nc.sync.dma_start(adj_cut[piece][:], late_rows[:, :, piece * PIECE : (piece + 1) * PIECE])
 
         identity = held.tile([P, P], BF16, name="identity")
         make_identity(nc, identity[:])
@@ -61,10 +61,12 @@ def tile_hode_mdp_kernel(tc, pe, w, b, adj, offs, out):
         h_t = [held.tile([P, CHUNK], BF16, name=f"h_t{c}") for c in range(CHUNKS)]
         sums = [sum_banks.tile([P, PIECE], F32, name=f"sum{piece}") for piece in range(PIECES)]
 
+        def pe_bf(c):
+            return pe_sb[c][:].bitcast(BF16).rearrange("p (s two) -> p s two", two=2)[:, :, 1]
+
         def gate(c):
-            halves = pe_sb[c][:].bitcast(BF16).rearrange("p (s two) -> p s two", two=2)
             gate_ps = gate_banks.tile([P, CHUNK], F32, name="gate_ps")
-            nc.tensor.matmul(gate_ps[:], w_sb[:], halves[:, :, 1], start=True, stop=True)
+            nc.tensor.matmul(gate_ps[:], w_sb[:], pe_bf(c), start=True, stop=True)
             nc.scalar.activation(sig[c][:], gate_ps[:], SIGMOID, bias=b_sb[:], scale=1.0)
 
         def multiply(c):
@@ -75,23 +77,30 @@ def tile_hode_mdp_kernel(tc, pe, w, b, adj, offs, out):
 
         def flip(c):
             flipped = flip_banks.tile([P, CHUNK], BF16, name="flipped")
+            if c < WHOLE_CHUNKS:
+                columns = h_bf[c][:].rearrange("p (q r) -> p r q", r=BLOCKS)
+            else:
+                columns = h_bf[c][:].rearrange("p (r q) -> p r q", r=BLOCKS)
             for r in range(BLOCKS):
-                nc.tensor.transpose(flipped[:, r * P : (r + 1) * P], h_bf[c][:, r * P : (r + 1) * P], identity[:])
+                nc.tensor.transpose(flipped[:, r * P : (r + 1) * P], columns[:, r, :], identity[:])
             nc.scalar.copy(h_t[c][:], flipped[:])
 
         zeros = held.tile([P, PIECE], BF16, name="zeros")
         nc.vector.memset(zeros[:], 0.0)
 
-        def warm_up():
-            for piece in range(PIECES):
-                nc.tensor.matmul(sums[piece][:], zeros[:, 0:P], zeros[:], start=True, stop=True)
+        early = held.tile([P, 1], F32, name="early")
+        nc.scalar.activation(early[:], zeros[:, 0:1], SIGMOID)
+
+        def warm_up(weights, moving, count):
+            for piece in range(count):
+                nc.tensor.matmul(sums[piece][:], weights, moving, start=True, stop=True)
 
         def add_to_sum(k, piece):
             c, r = divmod(k, BLOCKS)
-            if k < WHOLE_BLOCKS:
-                adj_part = adj_sb[k][:, piece * PIECE : (piece + 1) * PIECE]
+            if c < WHOLE_CHUNKS:
+                adj_part = adj_sb[c][:, r, piece * PIECE : (piece + 1) * PIECE]
             else:
-                adj_part = adj_cut[piece][:, k - WHOLE_BLOCKS, :]
+                adj_part = adj_cut[piece][:, k - EARLY_BLOCKS, :]
             nc.tensor.matmul(
                 sums[piece][:],
                 h_t[c][:, r * P : (r + 1) * P],
@@ -107,8 +116,10 @@ def tile_hode_mdp_kernel(tc, pe, w, b, adj, offs, out):
                 gate(t - 1)
             if 0 <= t - 2 < CHUNKS:
                 multiply(t - 2)
-            if t < 3:
-                warm_up()
+            if t == 0:
+                warm_up(zeros[:, 0:P], zeros[:], 4)
+            if t == 2:
+                warm_up(w_sb[:], pe_bf(1), 2)
             if 0 <= t - 4 < EARLY_BLOCKS:
                 for piece in range(PIECES):
                     add_to_sum(t - 4, piece)

@@ -22,6 +22,7 @@ K_BLOCKS = S // P
 LATE_CHUNKS = 2
 WHOLE_CHUNKS = CHUNKS - LATE_CHUNKS
 EARLY_BLOCKS = WHOLE_CHUNKS * BLOCKS
+ROUNDS = CHUNKS + 5
 
 FLOPS = 2 * P * P * S + 2 * P * S * N
 
@@ -41,12 +42,13 @@ def tile_hode_mdp_kernel(tc, pe, w, b, adj, offs, out):
         b_sb = held.tile([P, 1], F32, name="b_sb")
         nc.scalar.dma_start(b_sb[:], b)
         pe_sb = [held.tile([P, CHUNK], F32, name=f"pe{c}") for c in range(CHUNKS)]
-        for c in range(CHUNKS):
-            nc.sync.dma_start(pe_sb[c][:], pe[:, c * CHUNK : (c + 1) * CHUNK])
         adj_sb = [held.tile([P, BLOCKS, N], BF16, name=f"adj{c}") for c in range(WHOLE_CHUNKS)]
-        for c in range(WHOLE_CHUNKS):
-            rows = adj[c * CHUNK : (c + 1) * CHUNK, :]
-            nc.sync.dma_start(adj_sb[c][:], rows.rearrange("(p r) j -> p r j", r=BLOCKS))
+        for t in range(ROUNDS):
+            if 0 <= t - 1 < CHUNKS:
+                nc.sync.dma_start(pe_sb[t - 1][:], pe[:, (t - 1) * CHUNK : t * CHUNK])
+            if 0 <= t - 4 < WHOLE_CHUNKS:
+                rows = adj[(t - 4) * CHUNK : (t - 3) * CHUNK, :]
+                nc.sync.dma_start(adj_sb[t - 4][:], rows.rearrange("(p r) j -> p r j", r=BLOCKS))
         late_rows = adj[WHOLE_CHUNKS * CHUNK :, :].rearrange("(k p) j -> p k j", p=P)
         adj_cut = [held.tile([P, LATE_CHUNKS * BLOCKS, PIECE], BF16, name=f"adj_cut{piece}") for piece in range(PIECES)]
         for piece in range(PIECES):
@@ -109,7 +111,7 @@ def tile_hode_mdp_kernel(tc, pe, w, b, adj, offs, out):
                 stop=(k == K_BLOCKS - 1),
             )
 
-        for t in range(max(CHUNKS + 5, EARLY_BLOCKS + 4)):
+        for t in range(ROUNDS):
             if 0 <= t - 3 < CHUNKS:
                 flip(t - 3)
             if 0 <= t - 1 < CHUNKS:
@@ -118,11 +120,12 @@ def tile_hode_mdp_kernel(tc, pe, w, b, adj, offs, out):
                 multiply(t - 2)
             if t == 0:
                 warm_up(zeros[:, 0:P], zeros[:], 4)
-            if t == 2:
-                warm_up(w_sb[:], pe_bf(1), 2)
-            if 0 <= t - 4 < EARLY_BLOCKS:
-                for piece in range(PIECES):
-                    add_to_sum(t - 4, piece)
+            if 1 <= t <= 3:
+                warm_up(w_sb[:], pe_bf(t - 1), 2)
+            if 0 <= t - 4 < WHOLE_CHUNKS:
+                for k in range((t - 4) * BLOCKS, (t - 3) * BLOCKS):
+                    for piece in range(PIECES):
+                        add_to_sum(k, piece)
             if 0 <= t - 5 < CHUNKS:
                 fill_window(t - 5)
 

@@ -13,15 +13,17 @@ P = 128
 S = 2048
 N = 1024
 STEP = 0.4
-CHUNK = 256
-CHUNKS = S // CHUNK
-BLOCKS = CHUNK // P
-PIECE = 256
-PIECES = N // PIECE
-K_BLOCKS = S // P
-LATE_CHUNKS = 2
-WHOLE_CHUNKS = CHUNKS - LATE_CHUNKS
-EARLY_BLOCKS = WHOLE_CHUNKS * BLOCKS
+CHUNK_WIDTHS = (256, 256, 512, 512, 512)
+CHUNKS = len(CHUNK_WIDTHS)
+CHUNK_STARTS = [sum(CHUNK_WIDTHS[:c]) for c in range(CHUNKS)]
+LAST = CHUNKS - 1
+LATE_BLOCKS = 6
+EARLY_BLOCKS = S // P - LATE_BLOCKS
+PAIR = 2 * P
+QUARTER = N // 4
+PIECE_WIDTHS = (QUARTER, QUARTER, QUARTER, QUARTER // 2, QUARTER // 2)
+PIECES = len(PIECE_WIDTHS)
+PIECE_STARTS = [sum(PIECE_WIDTHS[:piece]) for piece in range(PIECES)]
 ROUNDS = CHUNKS + 5
 
 FLOPS = 2 * P * P * S + 2 * P * S * N
@@ -32,7 +34,7 @@ def tile_hode_mdp_kernel(tc, pe, w, b, adj, offs, out):
     with (
         tc.tile_pool(name="held", bufs=1) as held,
         tc.psum_pool(name="gate_banks", bufs=2) as gate_banks,
-        tc.psum_pool(name="flip_banks", bufs=2) as flip_banks,
+        tc.psum_pool(name="flip_banks", bufs=1) as flip_banks,
         tc.psum_pool(name="sum_banks", bufs=1) as sum_banks,
     ):
         offsets = held.tile([P, N // 16], U16, name="offsets")
@@ -41,33 +43,35 @@ def tile_hode_mdp_kernel(tc, pe, w, b, adj, offs, out):
         nc.scalar.dma_start(w_sb[:], w)
         b_sb = held.tile([P, 1], F32, name="b_sb")
         nc.scalar.dma_start(b_sb[:], b)
-        pe_sb = [held.tile([P, CHUNK], F32, name=f"pe{c}") for c in range(CHUNKS)]
-        adj_sb = [held.tile([P, BLOCKS, N], BF16, name=f"adj{c}") for c in range(WHOLE_CHUNKS)]
+        pe_sb = [held.tile([P, CHUNK_WIDTHS[c]], F32, name=f"pe{c}") for c in range(CHUNKS)]
+        adj_sb = [held.tile([P, 2, N], BF16, name=f"adj{g}") for g in range(CHUNK_STARTS[LAST] // PAIR)]
         for t in range(ROUNDS):
             if 0 <= t - 1 < CHUNKS:
-                nc.sync.dma_start(pe_sb[t - 1][:], pe[:, (t - 1) * CHUNK : t * CHUNK])
-            if 0 <= t - 4 < WHOLE_CHUNKS:
-                rows = adj[(t - 4) * CHUNK : (t - 3) * CHUNK, :]
-                nc.sync.dma_start(adj_sb[t - 4][:], rows.rearrange("(p r) j -> p r j", r=BLOCKS))
-        late_rows = adj[WHOLE_CHUNKS * CHUNK :, :].rearrange("(k p) j -> p k j", p=P)
-        adj_cut = [held.tile([P, LATE_CHUNKS * BLOCKS, PIECE], BF16, name=f"adj_cut{piece}") for piece in range(PIECES)]
-        for piece in range(PIECES):
-            nc.sync.dma_start(adj_cut[piece][:], late_rows[:, :, piece * PIECE : (piece + 1) * PIECE])
+                first = CHUNK_STARTS[t - 1]
+                nc.sync.dma_start(pe_sb[t - 1][:], pe[:, first : first + CHUNK_WIDTHS[t - 1]])
+            if 0 <= t - 4 < LAST:
+                for first in range(CHUNK_STARTS[t - 4], CHUNK_STARTS[t - 3], PAIR):
+                    rows = adj[first : first + PAIR, :].rearrange("(p r) j -> p r j", r=2)
+                    nc.sync.dma_start(adj_sb[first // PAIR][:], rows)
+        last_rows = adj[CHUNK_STARTS[LAST] :, :].rearrange("(k p) j -> p k j", p=P)
+        adj_cut = [held.tile([P, CHUNK_WIDTHS[LAST] // P, QUARTER], BF16, name=f"adj_cut{x}") for x in range(4)]
+        for x in range(4):
+            nc.sync.dma_start(adj_cut[x][:], last_rows[:, :, x * QUARTER : (x + 1) * QUARTER])
 
         identity = held.tile([P, P], BF16, name="identity")
         make_identity(nc, identity[:])
 
         h = held.tile([P, S], F32, name="h")
-        sig = [held.tile([P, CHUNK], F32, name=f"sig{c}") for c in range(CHUNKS)]
-        h_bf = [held.tile([P, CHUNK], BF16, name=f"h_bf{c}") for c in range(CHUNKS)]
-        h_t = [held.tile([P, CHUNK], BF16, name=f"h_t{c}") for c in range(CHUNKS)]
-        sums = [sum_banks.tile([P, PIECE], F32, name=f"sum{piece}") for piece in range(PIECES)]
+        sig = [held.tile([P, CHUNK_WIDTHS[c]], F32, name=f"sig{c}") for c in range(CHUNKS)]
+        h_bf = [held.tile([P, CHUNK_WIDTHS[c]], BF16, name=f"h_bf{c}") for c in range(CHUNKS)]
+        h_t = [held.tile([P, CHUNK_WIDTHS[c]], BF16, name=f"h_t{c}") for c in range(CHUNKS)]
+        sums = [sum_banks.tile([P, PIECE_WIDTHS[piece]], F32, name=f"sum{piece}") for piece in range(PIECES)]
 
         def pe_bf(c):
             return pe_sb[c][:].bitcast(BF16).rearrange("p (s two) -> p s two", two=2)[:, :, 1]
 
         def gate(c):
-            gate_ps = gate_banks.tile([P, CHUNK], F32, name="gate_ps")
+            gate_ps = gate_banks.tile([P, CHUNK_WIDTHS[c]], F32, name="gate_ps")
             nc.tensor.matmul(gate_ps[:], w_sb[:], pe_bf(c), start=True, stop=True)
             nc.scalar.activation(sig[c][:], gate_ps[:], SIGMOID, bias=b_sb[:], scale=1.0)
 
@@ -75,40 +79,46 @@ def tile_hode_mdp_kernel(tc, pe, w, b, adj, offs, out):
             nc.vector.tensor_tensor(h_bf[c][:], pe_sb[c][:], sig[c][:], MULT)
 
         def fill_window(c):
-            nc.vector.tensor_tensor(h[:, c * CHUNK : (c + 1) * CHUNK], pe_sb[c][:], sig[c][:], MULT)
+            first = CHUNK_STARTS[c]
+            nc.vector.tensor_tensor(h[:, first : first + CHUNK_WIDTHS[c]], pe_sb[c][:], sig[c][:], MULT)
 
         def flip(c):
-            flipped = flip_banks.tile([P, CHUNK], BF16, name="flipped")
-            if c < WHOLE_CHUNKS:
-                columns = h_bf[c][:].rearrange("p (q r) -> p r q", r=BLOCKS)
+            flipped = flip_banks.tile([P, CHUNK_WIDTHS[c]], BF16, name="flipped")
+            if c < LAST:
+                blocks = h_bf[c][:].rearrange("p (g q r) -> p g r q", q=P, r=2)
             else:
-                columns = h_bf[c][:].rearrange("p (r q) -> p r q", r=BLOCKS)
-            for r in range(BLOCKS):
-                nc.tensor.transpose(flipped[:, r * P : (r + 1) * P], columns[:, r, :], identity[:])
+                blocks = h_bf[c][:].rearrange("p (g r q) -> p g r q", q=P, r=2)
+            for k in range(CHUNK_WIDTHS[c] // P):
+                nc.tensor.transpose(flipped[:, k * P : (k + 1) * P], blocks[:, k // 2, k % 2, :], identity[:])
             nc.scalar.copy(h_t[c][:], flipped[:])
 
-        zeros = held.tile([P, PIECE], BF16, name="zeros")
+        zeros = held.tile([P, QUARTER], BF16, name="zeros")
         nc.vector.memset(zeros[:], 0.0)
 
         early = held.tile([P, 1], F32, name="early")
         nc.scalar.activation(early[:], zeros[:, 0:1], SIGMOID)
 
         def warm_up(weights, moving, count):
-            for piece in range(count):
-                nc.tensor.matmul(sums[piece][:], weights, moving, start=True, stop=True)
+            for i in range(count):
+                nc.tensor.matmul(sums[i % 3][:], weights, moving, start=True, stop=True)
+
+        chunk_of = [c for c in range(CHUNKS) for x in range(CHUNK_WIDTHS[c] // P)]
 
         def add_to_sum(k, piece):
-            c, r = divmod(k, BLOCKS)
-            if c < WHOLE_CHUNKS:
-                adj_part = adj_sb[c][:, r, piece * PIECE : (piece + 1) * PIECE]
+            c = chunk_of[k]
+            x = k - CHUNK_STARTS[c] // P
+            first, width = PIECE_STARTS[piece], PIECE_WIDTHS[piece]
+            if c < LAST:
+                adj_part = adj_sb[k // 2][:, k % 2, first : first + width]
             else:
-                adj_part = adj_cut[piece][:, k - EARLY_BLOCKS, :]
+                quarter, first = divmod(first, QUARTER)
+                adj_part = adj_cut[quarter][:, x, first : first + width]
             nc.tensor.matmul(
                 sums[piece][:],
-                h_t[c][:, r * P : (r + 1) * P],
+                h_t[c][:, x * P : (x + 1) * P],
                 adj_part,
                 start=(k == 0),
-                stop=(k == K_BLOCKS - 1),
+                stop=(k == len(chunk_of) - 1),
             )
 
         for t in range(ROUNDS):
@@ -120,21 +130,22 @@ def tile_hode_mdp_kernel(tc, pe, w, b, adj, offs, out):
                 multiply(t - 2)
             if t == 0:
                 warm_up(zeros[:, 0:P], zeros[:], 4)
-            if 1 <= t <= 3:
+            if 1 <= t <= 2:
                 warm_up(w_sb[:], pe_bf(t - 1), 2)
-            if 0 <= t - 4 < WHOLE_CHUNKS:
-                for k in range((t - 4) * BLOCKS, (t - 3) * BLOCKS):
+            for k in range(EARLY_BLOCKS):
+                if chunk_of[k] == t - 4:
                     for piece in range(PIECES):
                         add_to_sum(k, piece)
             if 0 <= t - 5 < CHUNKS:
                 fill_window(t - 5)
 
         for piece in range(PIECES):
-            for k in range(EARLY_BLOCKS, K_BLOCKS):
+            for k in range(EARLY_BLOCKS, len(chunk_of)):
                 add_to_sum(k, piece)
-            term = held.tile([P, PIECE], F32, name=f"term{piece}")
+            first, width = PIECE_STARTS[piece], PIECE_WIDTHS[piece]
+            term = held.tile([P, width], F32, name=f"term{piece}")
             nc.scalar.activation(term[:], sums[piece][:], COPY, scale=STEP)
-            result = held.tile([P, PIECE], F32, name=f"result{piece}")
-            listed = offsets[:, piece * (PIECE // 16) : (piece + 1) * (PIECE // 16)]
+            result = held.tile([P, width], F32, name=f"result{piece}")
+            listed = offsets[:, first // 16 : (first + width) // 16]
             nc.vector.tensor_tensor(result[:], h[:].indirect(listed), term[:], ADD)
-            nc.sync.dma_start(out[:, piece * PIECE : (piece + 1) * PIECE], result[:])
+            nc.sync.dma_start(out[:, first : first + width], result[:])

@@ -16,14 +16,13 @@ STEP = 0.4
 CHUNK_WIDTHS = (256, 256, 512, 512, 512)
 CHUNKS = len(CHUNK_WIDTHS)
 CHUNK_STARTS = [sum(CHUNK_WIDTHS[:c]) for c in range(CHUNKS)]
-LAST = CHUNKS - 1
 LATE_BLOCKS = 6
 EARLY_BLOCKS = S // P - LATE_BLOCKS
 PAIR = 2 * P
+PAIRS = S // PAIR
 QUARTER = N // 4
-PIECE_WIDTHS = (QUARTER, QUARTER, QUARTER, QUARTER // 2, QUARTER // 2)
-PIECES = len(PIECE_WIDTHS)
-PIECE_STARTS = [sum(PIECE_WIDTHS[:piece]) for piece in range(PIECES)]
+PIECE = QUARTER
+PIECES = N // PIECE
 ROUNDS = CHUNKS + 5
 
 FLOPS = 2 * P * P * S + 2 * P * S * N
@@ -34,7 +33,7 @@ def tile_hode_mdp_kernel(tc, pe, w, b, adj, offs, out):
     with (
         tc.tile_pool(name="held", bufs=1) as held,
         tc.psum_pool(name="gate_banks", bufs=2) as gate_banks,
-        tc.psum_pool(name="flip_banks", bufs=1) as flip_banks,
+        tc.psum_pool(name="flip_banks", bufs=2) as flip_banks,
         tc.psum_pool(name="sum_banks", bufs=1) as sum_banks,
     ):
         offsets = held.tile([P, N // 16], U16, name="offsets")
@@ -44,19 +43,19 @@ def tile_hode_mdp_kernel(tc, pe, w, b, adj, offs, out):
         b_sb = held.tile([P, 1], F32, name="b_sb")
         nc.scalar.dma_start(b_sb[:], b)
         pe_sb = [held.tile([P, CHUNK_WIDTHS[c]], F32, name=f"pe{c}") for c in range(CHUNKS)]
-        adj_sb = [held.tile([P, 2, N], BF16, name=f"adj{g}") for g in range(CHUNK_STARTS[LAST] // PAIR)]
+        adj_sb = [held.tile([P, 2, N], BF16, name=f"adj{g}") for g in range(PAIRS - 1)]
+        adj_rows = [adj[g * PAIR : (g + 1) * PAIR, :].rearrange("(p r) j -> p r j", r=2) for g in range(PAIRS)]
+        chunk_of = [c for c in range(CHUNKS) for x in range(CHUNK_WIDTHS[c] // P)]
+        for c in range(CHUNKS):
+            first = CHUNK_STARTS[c]
+            nc.sync.dma_start(pe_sb[c][:], pe[:, first : first + CHUNK_WIDTHS[c]])
         for t in range(ROUNDS):
-            if 0 <= t - 1 < CHUNKS:
-                first = CHUNK_STARTS[t - 1]
-                nc.sync.dma_start(pe_sb[t - 1][:], pe[:, first : first + CHUNK_WIDTHS[t - 1]])
-            if 0 <= t - 4 < LAST:
-                for first in range(CHUNK_STARTS[t - 4], CHUNK_STARTS[t - 3], PAIR):
-                    rows = adj[first : first + PAIR, :].rearrange("(p r) j -> p r j", r=2)
-                    nc.sync.dma_start(adj_sb[first // PAIR][:], rows)
-        last_rows = adj[CHUNK_STARTS[LAST] :, :].rearrange("(k p) j -> p k j", p=P)
-        adj_cut = [held.tile([P, CHUNK_WIDTHS[LAST] // P, QUARTER], BF16, name=f"adj_cut{x}") for x in range(4)]
+            for g in range(PAIRS - 1):
+                if chunk_of[2 * g] == t - 4:
+                    nc.sync.dma_start(adj_sb[g][:], adj_rows[g])
+        adj_cut = [held.tile([P, 2, QUARTER], BF16, name=f"adj_cut{x}") for x in range(4)]
         for x in range(4):
-            nc.sync.dma_start(adj_cut[x][:], last_rows[:, :, x * QUARTER : (x + 1) * QUARTER])
+            nc.sync.dma_start(adj_cut[x][:], adj_rows[PAIRS - 1][:, :, x * QUARTER : (x + 1) * QUARTER])
 
         identity = held.tile([P, P], BF16, name="identity")
         make_identity(nc, identity[:])
@@ -65,7 +64,7 @@ def tile_hode_mdp_kernel(tc, pe, w, b, adj, offs, out):
         sig = [held.tile([P, CHUNK_WIDTHS[c]], F32, name=f"sig{c}") for c in range(CHUNKS)]
         h_bf = [held.tile([P, CHUNK_WIDTHS[c]], BF16, name=f"h_bf{c}") for c in range(CHUNKS)]
         h_t = [held.tile([P, CHUNK_WIDTHS[c]], BF16, name=f"h_t{c}") for c in range(CHUNKS)]
-        sums = [sum_banks.tile([P, PIECE_WIDTHS[piece]], F32, name=f"sum{piece}") for piece in range(PIECES)]
+        sums = [sum_banks.tile([P, PIECE], F32, name=f"sum{piece}") for piece in range(PIECES)]
 
         def pe_bf(c):
             return pe_sb[c][:].bitcast(BF16).rearrange("p (s two) -> p s two", two=2)[:, :, 1]
@@ -84,10 +83,7 @@ def tile_hode_mdp_kernel(tc, pe, w, b, adj, offs, out):
 
         def flip(c):
             flipped = flip_banks.tile([P, CHUNK_WIDTHS[c]], BF16, name="flipped")
-            if c < LAST:
-                blocks = h_bf[c][:].rearrange("p (g q r) -> p g r q", q=P, r=2)
-            else:
-                blocks = h_bf[c][:].rearrange("p (g r q) -> p g r q", q=P, r=2)
+            blocks = h_bf[c][:].rearrange("p (g q r) -> p g r q", q=P, r=2)
             for k in range(CHUNK_WIDTHS[c] // P):
                 nc.tensor.transpose(flipped[:, k * P : (k + 1) * P], blocks[:, k // 2, k % 2, :], identity[:])
             nc.scalar.copy(h_t[c][:], flipped[:])
@@ -100,19 +96,15 @@ def tile_hode_mdp_kernel(tc, pe, w, b, adj, offs, out):
 
         def warm_up(weights, moving, count):
             for i in range(count):
-                nc.tensor.matmul(sums[i % 3][:], weights, moving, start=True, stop=True)
-
-        chunk_of = [c for c in range(CHUNKS) for x in range(CHUNK_WIDTHS[c] // P)]
+                nc.tensor.matmul(sums[i % PIECES][:], weights, moving, start=True, stop=True)
 
         def add_to_sum(k, piece):
             c = chunk_of[k]
             x = k - CHUNK_STARTS[c] // P
-            first, width = PIECE_STARTS[piece], PIECE_WIDTHS[piece]
-            if c < LAST:
-                adj_part = adj_sb[k // 2][:, k % 2, first : first + width]
+            if k // 2 < PAIRS - 1:
+                adj_part = adj_sb[k // 2][:, k % 2, piece * PIECE : (piece + 1) * PIECE]
             else:
-                quarter, first = divmod(first, QUARTER)
-                adj_part = adj_cut[quarter][:, x, first : first + width]
+                adj_part = adj_cut[piece][:, k % 2, :]
             nc.tensor.matmul(
                 sums[piece][:],
                 h_t[c][:, x * P : (x + 1) * P],
@@ -129,7 +121,7 @@ def tile_hode_mdp_kernel(tc, pe, w, b, adj, offs, out):
             if 0 <= t - 2 < CHUNKS:
                 multiply(t - 2)
             if t == 0:
-                warm_up(zeros[:, 0:P], zeros[:], 4)
+                warm_up(zeros[:, 0:P], zeros[:], 8)
             if 1 <= t <= 2:
                 warm_up(w_sb[:], pe_bf(t - 1), 2)
             for k in range(EARLY_BLOCKS):
@@ -142,10 +134,12 @@ def tile_hode_mdp_kernel(tc, pe, w, b, adj, offs, out):
         for piece in range(PIECES):
             for k in range(EARLY_BLOCKS, len(chunk_of)):
                 add_to_sum(k, piece)
-            first, width = PIECE_STARTS[piece], PIECE_WIDTHS[piece]
-            term = held.tile([P, width], F32, name=f"term{piece}")
-            nc.scalar.activation(term[:], sums[piece][:], COPY, scale=STEP)
-            result = held.tile([P, width], F32, name=f"result{piece}")
-            listed = offsets[:, first // 16 : (first + width) // 16]
-            nc.vector.tensor_tensor(result[:], h[:].indirect(listed), term[:], ADD)
-            nc.sync.dma_start(out[:, first : first + width], result[:])
+            width = PIECE if piece < PIECES - 1 else PIECE // 2
+            for first in range(0, PIECE, width):
+                term = held.tile([P, width], F32, name=f"term{piece}_{first}")
+                nc.scalar.activation(term[:], sums[piece][:, first : first + width], COPY, scale=STEP)
+                result = held.tile([P, width], F32, name=f"result{piece}_{first}")
+                j = piece * PIECE + first
+                listed = offsets[:, j // 16 : (j + width) // 16]
+                nc.vector.tensor_tensor(result[:], h[:].indirect(listed), term[:], ADD)
+                nc.sync.dma_start(out[:, j : j + width], result[:])

import concourse.mybir as mybir
from concourse.masks import make_identity

F32 = mybir.dt.float32
BF16 = mybir.dt.bfloat16
U16 = mybir.dt.uint16
ADD = mybir.AluOpType.add
MULT = mybir.AluOpType.mult
SIGMOID = mybir.ActivationFunctionType.Sigmoid
COPY = mybir.ActivationFunctionType.Copy

P = 128
S = 2048
N = 1024
STEP = 0.4
CHUNK_WIDTHS = (256, 256, 512, 512, 512)
CHUNKS = len(CHUNK_WIDTHS)
CHUNK_STARTS = [sum(CHUNK_WIDTHS[:c]) for c in range(CHUNKS)]
LATE_BLOCKS = 6
EARLY_BLOCKS = S // P - LATE_BLOCKS
PAIR = 2 * P
PAIRS = S // PAIR
QUARTER = N // 4
PIECE = QUARTER
PIECES = N // PIECE
ROUNDS = CHUNKS + 5

FLOPS = 2 * P * P * S + 2 * P * S * N


def tile_hode_mdp_kernel(tc, pe, w, b, adj, offs, out):
    nc = tc.nc
    with (
        tc.tile_pool(name="held", bufs=1) as held,
        tc.psum_pool(name="gate_banks", bufs=2) as gate_banks,
        tc.psum_pool(name="flip_banks", bufs=2) as flip_banks,
        tc.psum_pool(name="sum_banks", bufs=1) as sum_banks,
    ):
        offsets = held.tile([P, N // 16], U16, name="offsets")
        nc.sync.dma_start(offsets[:], offs)
        w_sb = held.tile([P, P], BF16, name="w_sb")
        nc.scalar.dma_start(w_sb[:], w)
        b_sb = held.tile([P, 1], F32, name="b_sb")
        nc.scalar.dma_start(b_sb[:], b)
        pe_sb = [held.tile([P, CHUNK_WIDTHS[c]], F32, name=f"pe{c}") for c in range(CHUNKS)]
        adj_sb = [held.tile([P, 2, N], BF16, name=f"adj{g}") for g in range(PAIRS - 1)]
        adj_rows = [adj[g * PAIR : (g + 1) * PAIR, :].rearrange("(p r) j -> p r j", r=2) for g in range(PAIRS)]
        chunk_of = [c for c in range(CHUNKS) for x in range(CHUNK_WIDTHS[c] // P)]
        for c in range(CHUNKS):
            first = CHUNK_STARTS[c]
            nc.sync.dma_start(pe_sb[c][:], pe[:, first : first + CHUNK_WIDTHS[c]])
        for t in range(ROUNDS):
            for g in range(PAIRS - 1):
                if chunk_of[2 * g] == t - 4:
                    nc.sync.dma_start(adj_sb[g][:], adj_rows[g])
        adj_cut = [held.tile([P, 2, QUARTER], BF16, name=f"adj_cut{x}") for x in range(4)]
        for x in range(4):
            nc.sync.dma_start(adj_cut[x][:], adj_rows[PAIRS - 1][:, :, x * QUARTER : (x + 1) * QUARTER])

        identity = held.tile([P, P], BF16, name="identity")
        make_identity(nc, identity[:])

        h = held.tile([P, S], F32, name="h")
        sig = [held.tile([P, CHUNK_WIDTHS[c]], F32, name=f"sig{c}") for c in range(CHUNKS)]
        h_bf = [held.tile([P, CHUNK_WIDTHS[c]], BF16, name=f"h_bf{c}") for c in range(CHUNKS)]
        h_t = [held.tile([P, CHUNK_WIDTHS[c]], BF16, name=f"h_t{c}") for c in range(CHUNKS)]
        sums = [sum_banks.tile([P, PIECE], F32, name=f"sum{piece}") for piece in range(PIECES)]

        def pe_bf(c):
            return pe_sb[c][:].bitcast(BF16).rearrange("p (s two) -> p s two", two=2)[:, :, 1]

        def gate(c):
            gate_ps = gate_banks.tile([P, CHUNK_WIDTHS[c]], F32, name="gate_ps")
            nc.tensor.matmul(gate_ps[:], w_sb[:], pe_bf(c), start=True, stop=True)
            nc.scalar.activation(sig[c][:], gate_ps[:], SIGMOID, bias=b_sb[:], scale=1.0)

        def multiply(c):
            nc.vector.tensor_tensor(h_bf[c][:], pe_sb[c][:], sig[c][:], MULT)

        def fill_window(c):
            first = CHUNK_STARTS[c]
            nc.vector.tensor_tensor(h[:, first : first + CHUNK_WIDTHS[c]], pe_sb[c][:], sig[c][:], MULT)

        def flip(c):
            flipped = flip_banks.tile([P, CHUNK_WIDTHS[c]], BF16, name="flipped")
            blocks = h_bf[c][:].rearrange("p (g q r) -> p g r q", q=P, r=2)
            for k in range(CHUNK_WIDTHS[c] // P):
                nc.tensor.transpose(flipped[:, k * P : (k + 1) * P], blocks[:, k // 2, k % 2, :], identity[:])
            nc.scalar.copy(h_t[c][:], flipped[:])

        zeros = held.tile([P, QUARTER], BF16, name="zeros")
        nc.vector.memset(zeros[:], 0.0)

        early = held.tile([P, 1], F32, name="early")
        nc.scalar.activation(early[:], zeros[:, 0:1], SIGMOID)

        def warm_up(weights, moving, count):
            for i in range(count):
                nc.tensor.matmul(sums[i % PIECES][:], weights, moving, start=True, stop=True)

        def add_to_sum(k, piece):
            c = chunk_of[k]
            x = k - CHUNK_STARTS[c] // P
            if k // 2 < PAIRS - 1:
                adj_part = adj_sb[k // 2][:, k % 2, piece * PIECE : (piece + 1) * PIECE]
            else:
                adj_part = adj_cut[piece][:, k % 2, :]
            nc.tensor.matmul(
                sums[piece][:],
                h_t[c][:, x * P : (x + 1) * P],
                adj_part,
                start=(k == 0),
                stop=(k == len(chunk_of) - 1),
            )

        for t in range(ROUNDS):
            if 0 <= t - 3 < CHUNKS:
                flip(t - 3)
            if 0 <= t - 1 < CHUNKS:
                gate(t - 1)
            if 0 <= t - 2 < CHUNKS:
                multiply(t - 2)
            if t == 0:
                warm_up(zeros[:, 0:P], zeros[:], 8)
            if 1 <= t <= 2:
                warm_up(w_sb[:], pe_bf(t - 1), 2)
            for k in range(EARLY_BLOCKS):
                if chunk_of[k] == t - 4:
                    for piece in range(PIECES):
                        add_to_sum(k, piece)
            if 0 <= t - 5 < CHUNKS:
                fill_window(t - 5)

        for piece in range(PIECES):
            for k in range(EARLY_BLOCKS, len(chunk_of)):
                add_to_sum(k, piece)
            width = PIECE if piece < PIECES - 1 else PIECE // 2
            for first in range(0, PIECE, width):
                term = held.tile([P, width], F32, name=f"term{piece}_{first}")
                nc.scalar.activation(term[:], sums[piece][:, first : first + width], COPY, scale=STEP)
                result = held.tile([P, width], F32, name=f"result{piece}_{first}")
                j = piece * PIECE + first
                listed = offsets[:, j // 16 : (j + width) // 16]
                nc.vector.tensor_tensor(result[:], h[:].indirect(listed), term[:], ADD)
                nc.sync.dma_start(out[:, j : j + width], result[:])
